import numpy as np
import ml_dtypes


def mxq(x, axis, fmt="e4m3"):
    dtype, down = {"e4m3": (ml_dtypes.float8_e4m3fn, 7), "e5m2": (ml_dtypes.float8_e5m2, 14)}[fmt]
    v = np.moveaxis(np.asarray(x, np.float32).astype(ml_dtypes.bfloat16).astype(np.float64), axis, -1)
    blocks = v.reshape(v.shape[:-1] + (-1, 32))
    amax = np.abs(blocks).max(-1, keepdims=True)
    byte = np.maximum(np.where(amax > 0, np.frexp(amax)[1] - 1 + 127, 0) - down, 1)
    scale = np.exp2(byte - 127.0)
    codes = (blocks / scale).astype(np.float32).astype(dtype).astype(np.float64)
    return np.moveaxis((codes * scale).reshape(v.shape), -1, axis)


WIDE = False


def mx_kscale(k):
    if not WIDE:
        return np.ones(k)
    levels = np.array([10, -10, 5, -5, 0])
    a = np.random.permutation(np.resize(levels, k // 512 * 4)).reshape(k // 512, 4)
    idx = np.arange(k)
    return np.exp2(a[idx // 512, idx % 128 // 32])


BF16 = ml_dtypes.bfloat16


def bf(x):
    return np.asarray(x, np.float32).astype(BF16)


def f64(x):
    return np.asarray(x).astype(np.float64)


B, C, K, L, R = 4, 64, 512, 16, 128


def transition():
    g = np.exp(2.5 * np.random.standard_normal((K, K)))
    return g / g.sum(1, keepdims=True)


def setup_inputs():
    s = mx_kscale(K)
    x = np.random.standard_normal((B, C, K, L)) * 2.0 * s[None, None, :, None]
    return {'x': bf(x.reshape(B, C, K * L)),
            'support0': bf(transition() * s[:, None] / s[None, :]),
            'support1': bf(transition() * s[:, None] / s[None, :])}


def two_hops(xq, a):
    aq = mxq(f64(a).T, 0, 'e4m3')
    x1 = xq @ aq
    x2 = mxq(x1, 2, 'e4m3') @ aq
    return x1, x2


def reference(x, support0, support1):
    xr = f64(x).reshape(B, C, K, L).transpose(0, 3, 1, 2).reshape(B * L, C, K)
    xq = mxq(xr, 2, 'e4m3')
    f1, f2 = two_hops(xq, support0)
    g1, g2 = two_hops(xq, support1)
    return f1, f2, g1, g2

@@ -1,0 +1,259 @@
+from contextlib import ExitStack
+
+import concourse.mybir as mybir
+from concourse.masks import make_identity
+
+BF16 = mybir.dt.bfloat16
+F32 = mybir.dt.float32
+U32 = mybir.dt.uint32
+U8 = mybir.dt.uint8
+FP8X4 = mybir.dt.float8_e4m3fn_x4
+
+P = 128
+PACK = 4
+BATCHES, CHANNELS, NODES, STEPS = 4, 64, 512, 16
+assert NODES == P * PACK
+
+ROWS = 4
+PANEL_STEPS = P * ROWS // CHANNELS
+PANEL = P * ROWS
+STEP_PAIRS = PANEL_STEPS // 2
+SLABS = (BATCHES // 2) * (STEPS // PANEL_STEPS)
+HALF = NODES // 2
+LAG = 6
+
+FLOPS = 4 * 2 * BATCHES * STEPS * CHANNELS * NODES * NODES
+
+
+def tile_adaptivegcn_pb_t_kernel(
+    tc, x, support0, support1, out_0, out_1, out_2, out_3
+):
+    nc = tc.nc
+    supports = (support0, support1)
+    hop1_outs = (out_0, out_2)
+    hop2_outs = (out_1, out_3)
+
+    with ExitStack() as ctx:
+        ctx.enter_context(tc.manual_schedule())
+        resident = ctx.enter_context(tc.tile_pool(name="resident", bufs=1))
+        x_pool = ctx.enter_context(tc.tile_pool(name="x_pool", bufs=2))
+        hop1_pool = ctx.enter_context(tc.tile_pool(name="hop1_pool", bufs=3))
+        store_pool = ctx.enter_context(tc.tile_pool(name="store_pool", bufs=6))
+        psum_quant = ctx.enter_context(tc.psum_pool(name="psum_quant", bufs=4))
+        psum_store = ctx.enter_context(tc.psum_pool(name="psum_store", bufs=4))
+
+        def load_support(s):
+            rows = resident.tile([P, PACK, NODES], BF16, name="support_rows_%d" % s)
+            nc.sync.dma_start(
+                out=rows[:], in_=supports[s].rearrange("(g p) v -> p g v", p=P)
+            )
+            return rows
+
+        def load_x(pair):
+            rows = x[2 * pair : 2 * pair + 2].rearrange("b c f -> (b c) f")
+            pieces = []
+            for t in range(PACK):
+                piece = resident.tile([P, P * STEPS], BF16, name="x_rows_%d_%d" % (pair, t))
+                nc.sync.dma_start(
+                    out=piece[:], in_=rows[:, t * P * STEPS : (t + 1) * P * STEPS]
+                )
+                pieces.append(piece)
+            return pieces
+
+        support_rows = {}
+        x_rows = {}
+        support_rows[0] = load_support(0)
+        x_rows[0] = load_x(0)
+        support_rows[1] = load_support(1)
+        x_rows[1] = load_x(1)
+
+        ident_bf16 = resident.tile([P, P], BF16)
+        make_identity(nc, ident_bf16[:])
+        ident_f32 = resident.tile([P, P], F32)
+        make_identity(nc, ident_f32[:])
+
+        support_codes = {}
+        support_scales = {}
+
+        def quantise_support(s):
+            grouped = resident.tile(
+                [P, NODES, PACK], BF16, name="support_grouped_%d" % s, align_bytes=64
+            )
+            for half in range(2):
+                flipped = psum_store.tile([P, PACK, HALF], BF16, tag="store_bank")
+                for t in range(PACK):
+                    for g in range(2):
+                        nc.tensor.transpose(
+                            flipped[:, t, g * P : (g + 1) * P],
+                            support_rows[s][:, 2 * half + g, t * P : (t + 1) * P],
+                            ident_bf16[:],
+                        )
+                copy = nc.vector.tensor_copy if half == 0 else nc.scalar.copy
+                copy(
+                    out=grouped[:, half * HALF : (half + 1) * HALF, :],
+                    in_=flipped[:].rearrange("p t w -> p w t"),
+                )
+            support_codes[s] = resident.tile(
+                [P, NODES], U32, name="support_codes_%d" % s, align_bytes=64
+            )
+            support_scales[s] = resident.tile(
+                [P, NODES], U8, name="support_scales_%d" % s, align_bytes=64
+            )
+            nc.vector.quantize_mx(
+                out=support_codes[s][:].bitcast(FP8X4),
+                scales=support_scales[s][:],
+                in_=grouped[:].rearrange("p w t -> p (w t)"),
+            )
+
+        x_grouped = {}
+        x_codes = {}
+        x_scales = {}
+
+        def new_slab(slab):
+            x_grouped[slab] = x_pool.tile(
+                [P, 2, ROWS, PANEL_STEPS, CHANNELS // ROWS, PACK],
+                BF16,
+                name="x_grouped",
+                align_bytes=64,
+            )
+            x_codes[slab] = x_pool.tile([P, 2, PANEL], U32, name="x_codes", align_bytes=64)
+            x_scales[slab] = x_pool.tile([P, 2, PANEL], U8, name="x_scales", align_bytes=64)
+
+        def flip_x(slab, step_pairs):
+            pair, half = divmod(slab, STEPS // PANEL_STEPS)
+            banks = {}
+            for i in step_pairs:
+                banks[i] = psum_quant.tile([P, PACK, P], F32, name="x_flipped", tag="quant_bank")
+            for t in range(PACK):
+                words = x_rows[pair][t][:].bitcast(F32).rearrange(
+                    "q (k w) -> q k w", w=STEPS // 2
+                )
+                for i in step_pairs:
+                    nc.tensor.transpose(
+                        banks[i][:, t, :], words[:, :, half * STEP_PAIRS + i], ident_f32[:]
+                    )
+            return banks
+
+        def sort_x(copy, slab, i, bank):
+            halves = bank[:].bitcast(BF16).rearrange(
+                "p t (b c j e) -> p e b j c t", b=2, c=CHANNELS // ROWS, j=ROWS, e=2
+            )
+            for e in range(2):
+                copy(out=x_grouped[slab][:, :, :, 2 * i + e, :, :], in_=halves[:, e])
+
+        def quantise_x(slab, b):
+            nc.vector.quantize_mx(
+                out=x_codes[slab][:, b, :].bitcast(FP8X4),
+                scales=x_scales[slab][:, b, :],
+                in_=x_grouped[slab][:, b].rearrange("p j l c t -> p (j l c t)"),
+            )
+
+        def panel_in_hbm(out, slab, b):
+            pair, half = divmod(slab, STEPS // PANEL_STEPS)
+            first = (2 * pair + b) * STEPS + half * PANEL_STEPS
+            return out[first : first + PANEL_STEPS].rearrange("l (c j) w -> (l c) (j w)", j=ROWS)
+
+        def product_to_hbm(codes, scales, s, j, staged, panel):
+            cols = slice(j * P, (j + 1) * P)
+            bank = psum_store.tile([P, NODES], F32, tag="store_bank")
+            nc.tensor.matmul_mx(
+                out=bank[:],
+                lhsT=codes[:, cols].bitcast(FP8X4),
+                lhsT_scale=scales[:, cols],
+                rhs=support_codes[s][:].bitcast(FP8X4),
+                rhs_scale=support_scales[s][:],
+                start=True,
+                stop=True,
+            )
+            nc.scalar.copy(out=staged[:, j, :], in_=bank[:])
+            if j == ROWS - 1:
+                nc.sync.dma_start(out=panel, in_=staged[:].rearrange("p j w -> p (j w)"))
+
+        def flipped_first_hop(slab, s, b, j, grouped):
+            cols = slice(j * P, (j + 1) * P)
+            bank = psum_quant.tile([P, PACK, P], F32, name="hop1_flipped", tag="quant_bank")
+            for t in range(PACK):
+                nodes = slice(t * P, (t + 1) * P)
+                nc.tensor.matmul_mx(
+                    out=bank[:, t, :],
+                    lhsT=support_codes[s][:, nodes].bitcast(FP8X4),
+                    lhsT_scale=support_scales[s][:, nodes],
+                    rhs=x_codes[slab][:, b, cols].bitcast(FP8X4),
+                    rhs_scale=x_scales[slab][:, b, cols],
+                    start=True,
+                    stop=True,
+                )
+            nc.vector.tensor_copy(out=grouped[:, cols, :], in_=bank[:].rearrange("p t r -> p r t"))
+
+        quantise_support(0)
+        new_slab(0)
+        first_banks = flip_x(0, range(STEP_PAIRS))
+        for i in range(STEP_PAIRS):
+            sort_x(nc.vector.tensor_copy if i % 2 == 0 else nc.scalar.copy, 0, i, first_banks[i])
+        quantise_x(0, 0)
+        quantise_x(0, 1)
+        quantise_support(1)
+
+        jobs = [(slab, s, b) for slab in range(SLABS) for s in range(2) for b in range(2)]
+        assert len(jobs) == SLABS * STEP_PAIRS
+        quarters = len(jobs) * ROWS
+        hop1_staged = {}
+        hop2_staged = {}
+        hop1_grouped = {}
+        hop1_codes = {}
+        hop1_scales = {}
+        for n in range(quarters + LAG):
+            if n < quarters:
+                job, j = divmod(n, ROWS)
+                slab, s, b = jobs[job]
+                i = job % STEP_PAIRS
+                if j == 0 and slab + 1 < SLABS:
+                    if i == 0:
+                        new_slab(slab + 1)
+                    sort_x(nc.vector.tensor_copy, slab + 1, i, flip_x(slab + 1, [i])[i])
+                if j == 0:
+                    hop1_staged[job] = store_pool.tile([P, ROWS, NODES], F32, name="staged")
+                product_to_hbm(
+                    x_codes[slab][:, b, :],
+                    x_scales[slab][:, b, :],
+                    s,
+                    j,
+                    hop1_staged[job],
+                    panel_in_hbm(hop1_outs[s], slab, b),
+                )
+            if n >= LAG:
+                job, j = divmod(n - LAG, ROWS)
+                slab, s, b = jobs[job]
+                if j == 0:
+                    hop2_staged[job] = store_pool.tile([P, ROWS, NODES], F32, name="staged")
+                product_to_hbm(
+                    hop1_codes[job][:],
+                    hop1_scales[job][:],
+                    s,
+                    j,
+                    hop2_staged[job],
+                    panel_in_hbm(hop2_outs[s], slab, b),
+                )
+            if n < quarters:
+                job, j = divmod(n, ROWS)
+                slab, s, b = jobs[job]
+                i = job % STEP_PAIRS
+                if j == 0:
+                    hop1_grouped[job] = hop1_pool.tile(
+                        [P, PANEL, PACK], BF16, name="hop1_grouped", align_bytes=64
+                    )
+                flipped_first_hop(slab, s, b, j, hop1_grouped[job])
+                if j == ROWS - 1:
+                    hop1_codes[job] = hop1_pool.tile(
+                        [P, PANEL], U32, name="hop1_codes", align_bytes=64
+                    )
+                    hop1_scales[job] = hop1_pool.tile(
+                        [P, PANEL], U8, name="hop1_scales", align_bytes=64
+                    )
+                    nc.vector.quantize_mx(
+                        out=hop1_codes[job][:].bitcast(FP8X4),
+                        scales=hop1_scales[job][:],
+                        in_=hop1_grouped[job][:].rearrange("p r t -> p (r t)"),
+                    )
+                if i == STEP_PAIRS - 1 and j in (1, 2) and slab + 1 < SLABS:
+                    quantise_x(slab + 1, j - 1)

@@ -13,12 +13,13 @@ P = 128
 PACK = 4
 BATCHES, CHANNELS, NODES, STEPS = 4, 64, 512, 16
 assert NODES == P * PACK
+assert 2 * CHANNELS == P
 
 ROWS = 4
-PANEL_STEPS = P * ROWS // CHANNELS
 PANEL = P * ROWS
-STEP_PAIRS = PANEL_STEPS // 2
-SLABS = (BATCHES // 2) * (STEPS // PANEL_STEPS)
+PANEL_STEPS = PANEL // CHANNELS
+PANELS = STEPS // PANEL_STEPS
+X_BANKS = 4
 HALF = NODES // 2
 LAG = 6
 
@@ -44,38 +45,38 @@ def tile_adaptivegcn_pb_t_kernel(
 
         def load_support(s):
             rows = resident.tile([P, PACK, NODES], BF16, name="support_rows_%d" % s)
-            nc.sync.dma_start(
-                out=rows[:], in_=supports[s].rearrange("(g p) v -> p g v", p=P)
-            )
+            nc.sync.dma_start(out=rows[:], in_=supports[s].rearrange("(g p) v -> p g v", p=P))
             return rows
 
-        def load_x(pair):
-            rows = x[2 * pair : 2 * pair + 2].rearrange("b c f -> (b c) f")
+        def load_x(batch):
+            rows = x[batch].rearrange("c (h f) -> (c h) f", h=2)
             pieces = []
-            for t in range(PACK):
-                piece = resident.tile([P, P * STEPS], BF16, name="x_rows_%d_%d" % (pair, t))
-                nc.sync.dma_start(
-                    out=piece[:], in_=rows[:, t * P * STEPS : (t + 1) * P * STEPS]
-                )
+            for u in range(2):
+                piece = resident.tile([P, P * STEPS], BF16, name="x_rows_%d_%d" % (batch, u))
+                nc.sync.dma_start(out=piece[:], in_=rows[:, u * P * STEPS : (u + 1) * P * STEPS])
                 pieces.append(piece)
             return pieces
 
-        support_rows = {}
-        x_rows = {}
-        support_rows[0] = load_support(0)
-        x_rows[0] = load_x(0)
+        support_rows = {0: load_support(0)}
+        x_rows = {0: load_x(0)}
         support_rows[1] = load_support(1)
-        x_rows[1] = load_x(1)
+        for batch in range(1, BATCHES):
+            x_rows[batch] = load_x(batch)
 
         ident_bf16 = resident.tile([P, P], BF16)
         make_identity(nc, ident_bf16[:])
         ident_f32 = resident.tile([P, P], F32)
         make_identity(nc, ident_f32[:])
+        sort_channels = resident.tile([P, P], F32)
+        nc.vector.tensor_copy(
+            out=sort_channels[:].rearrange("q (j c h) -> q j c h", j=ROWS, h=2),
+            in_=ident_f32[:].rearrange("q (c j h) -> q j c h", j=ROWS, h=2),
+        )
 
         support_codes = {}
         support_scales = {}
 
-        def quantise_support(s):
+        def quantise_support(s, copies):
             grouped = resident.tile(
                 [P, NODES, PACK], BF16, name="support_grouped_%d" % s, align_bytes=64
             )
@@ -88,8 +89,7 @@ def tile_adaptivegcn_pb_t_kernel(
                             support_rows[s][:, 2 * half + g, t * P : (t + 1) * P],
                             ident_bf16[:],
                         )
-                copy = nc.vector.tensor_copy if half == 0 else nc.scalar.copy
-                copy(
+                copies[half](
                     out=grouped[:, half * HALF : (half + 1) * HALF, :],
                     in_=flipped[:].rearrange("p t w -> p w t"),
                 )
@@ -109,51 +109,42 @@ def tile_adaptivegcn_pb_t_kernel(
         x_codes = {}
         x_scales = {}
 
-        def new_slab(slab):
-            x_grouped[slab] = x_pool.tile(
-                [P, 2, ROWS, PANEL_STEPS, CHANNELS // ROWS, PACK],
-                BF16,
-                name="x_grouped",
-                align_bytes=64,
+        def new_batch(batch):
+            x_grouped[batch] = x_pool.tile(
+                [P, PANELS, PANEL * PACK], BF16, name="x_grouped", align_bytes=64
             )
-            x_codes[slab] = x_pool.tile([P, 2, PANEL], U32, name="x_codes", align_bytes=64)
-            x_scales[slab] = x_pool.tile([P, 2, PANEL], U8, name="x_scales", align_bytes=64)
+            x_codes[batch] = x_pool.tile([P, PANELS, PANEL], U32, name="x_codes", align_bytes=64)
+            x_scales[batch] = x_pool.tile([P, PANELS, PANEL], U8, name="x_scales", align_bytes=64)
 
-        def flip_x(slab, step_pairs):
-            pair, half = divmod(slab, STEPS // PANEL_STEPS)
+        def flip_x(batch, which_banks):
             banks = {}
-            for i in step_pairs:
-                banks[i] = psum_quant.tile([P, PACK, P], F32, name="x_flipped", tag="quant_bank")
-            for t in range(PACK):
-                words = x_rows[pair][t][:].bitcast(F32).rearrange(
-                    "q (k w) -> q k w", w=STEPS // 2
-                )
-                for i in step_pairs:
-                    nc.tensor.transpose(
-                        banks[i][:, t, :], words[:, :, half * STEP_PAIRS + i], ident_f32[:]
-                    )
+            for g in which_banks:
+                banks[g] = psum_quant.tile([P, 2, 2, P], F32, name="x_flipped", tag="quant_bank")
+            for u in range(2):
+                words = x_rows[batch][u][:].bitcast(F32).rearrange("q (k w) -> q k w", w=STEPS // 2)
+                for g in which_banks:
+                    for i in range(2):
+                        nc.tensor.transpose(
+                            banks[g][:, i, u, :], words[:, :, 2 * g + i], sort_channels[:]
+                        )
             return banks
 
-        def sort_x(copy, slab, i, bank):
-            halves = bank[:].bitcast(BF16).rearrange(
-                "p t (b c j e) -> p e b j c t", b=2, c=CHANNELS // ROWS, j=ROWS, e=2
+        def sort_x(copy, batch, g, bank):
+            halves = bank[:].bitcast(BF16).rearrange("p i u (j m e) -> p e i j m u", j=ROWS, e=2)
+            sorted_steps = x_grouped[batch][:, g // 2, :].rearrange(
+                "p (j a i e m u) -> p a e i j m u", j=ROWS, a=2, i=2, e=2, u=2
             )
             for e in range(2):
-                copy(out=x_grouped[slab][:, :, :, 2 * i + e, :, :], in_=halves[:, e])
+                copy(out=sorted_steps[:, g % 2, e], in_=halves[:, e])
 
-        def quantise_x(slab, b):
+        def quantise_x(batch, panel):
             nc.vector.quantize_mx(
-                out=x_codes[slab][:, b, :].bitcast(FP8X4),
-                scales=x_scales[slab][:, b, :],
-                in_=x_grouped[slab][:, b].rearrange("p j l c t -> p (j l c t)"),
+                out=x_codes[batch][:, panel, :].bitcast(FP8X4),
+                scales=x_scales[batch][:, panel, :],
+                in_=x_grouped[batch][:, panel, :],
             )
 
-        def panel_in_hbm(out, slab, b):
-            pair, half = divmod(slab, STEPS // PANEL_STEPS)
-            first = (2 * pair + b) * STEPS + half * PANEL_STEPS
-            return out[first : first + PANEL_STEPS].rearrange("l (c j) w -> (l c) (j w)", j=ROWS)
-
-        def product_to_hbm(codes, scales, s, j, staged, panel):
+        def product_to_hbm(codes, scales, s, j, staged, out, batch, panel):
             cols = slice(j * P, (j + 1) * P)
             bank = psum_store.tile([P, NODES], F32, tag="store_bank")
             nc.tensor.matmul_mx(
@@ -167,9 +158,15 @@ def tile_adaptivegcn_pb_t_kernel(
             )
             nc.scalar.copy(out=staged[:, j, :], in_=bank[:])
             if j == ROWS - 1:
-                nc.sync.dma_start(out=panel, in_=staged[:].rearrange("p j w -> p (j w)"))
+                first = batch * STEPS + panel * PANEL_STEPS
+                nc.sync.dma_start(
+                    out=out[first : first + PANEL_STEPS].rearrange(
+                        "l (c j) w -> (l c) (j w)", j=ROWS
+                    ),
+                    in_=staged[:].rearrange("p j w -> p (j w)"),
+                )
 
-        def flipped_first_hop(slab, s, b, j, grouped):
+        def flipped_first_hop(batch, s, panel, j, grouped):
             cols = slice(j * P, (j + 1) * P)
             bank = psum_quant.tile([P, PACK, P], F32, name="hop1_flipped", tag="quant_bank")
             for t in range(PACK):
@@ -178,71 +175,72 @@ def tile_adaptivegcn_pb_t_kernel(
                     out=bank[:, t, :],
                     lhsT=support_codes[s][:, nodes].bitcast(FP8X4),
                     lhsT_scale=support_scales[s][:, nodes],
-                    rhs=x_codes[slab][:, b, cols].bitcast(FP8X4),
-                    rhs_scale=x_scales[slab][:, b, cols],
+                    rhs=x_codes[batch][:, panel, cols].bitcast(FP8X4),
+                    rhs_scale=x_scales[batch][:, panel, cols],
                     start=True,
                     stop=True,
                 )
             nc.vector.tensor_copy(out=grouped[:, cols, :], in_=bank[:].rearrange("p t r -> p r t"))
 
-        quantise_support(0)
-        new_slab(0)
-        first_banks = flip_x(0, range(STEP_PAIRS))
-        for i in range(STEP_PAIRS):
-            sort_x(nc.vector.tensor_copy if i % 2 == 0 else nc.scalar.copy, 0, i, first_banks[i])
-        quantise_x(0, 0)
-        quantise_x(0, 1)
-        quantise_support(1)
+        quantise_support(0, (nc.vector.tensor_copy, nc.scalar.copy))
+        new_batch(0)
+        first_banks = flip_x(0, range(X_BANKS))
+        for panel in range(PANELS):
+            sort_x(nc.vector.tensor_copy, 0, 2 * panel, first_banks[2 * panel])
+            sort_x(nc.scalar.copy, 0, 2 * panel + 1, first_banks[2 * panel + 1])
+            quantise_x(0, panel)
 
-        jobs = [(slab, s, b) for slab in range(SLABS) for s in range(2) for b in range(2)]
-        assert len(jobs) == SLABS * STEP_PAIRS
+        jobs = [
+            (batch, s, panel)
+            for batch in range(BATCHES)
+            for s in range(2)
+            for panel in range(PANELS)
+        ]
+        assert len(jobs) == BATCHES * X_BANKS
         quarters = len(jobs) * ROWS
-        hop1_staged = {}
-        hop2_staged = {}
+        staging = {}
         hop1_grouped = {}
         hop1_codes = {}
         hop1_scales = {}
         for n in range(quarters + LAG):
             if n < quarters:
                 job, j = divmod(n, ROWS)
-                slab, s, b = jobs[job]
-                i = job % STEP_PAIRS
-                if j == 0 and slab + 1 < SLABS:
-                    if i == 0:
-                        new_slab(slab + 1)
-                    sort_x(nc.vector.tensor_copy, slab + 1, i, flip_x(slab + 1, [i])[i])
+                batch, s, panel = jobs[job]
                 if j == 0:
-                    hop1_staged[job] = store_pool.tile([P, ROWS, NODES], F32, name="staged")
+                    staging[1, job] = store_pool.tile([P, ROWS, NODES], F32, name="staged")
                 product_to_hbm(
-                    x_codes[slab][:, b, :],
-                    x_scales[slab][:, b, :],
+                    x_codes[batch][:, panel, :],
+                    x_scales[batch][:, panel, :],
                     s,
                     j,
-                    hop1_staged[job],
-                    panel_in_hbm(hop1_outs[s], slab, b),
+                    staging[1, job],
+                    hop1_outs[s],
+                    batch,
+                    panel,
                 )
             if n >= LAG:
                 job, j = divmod(n - LAG, ROWS)
-                slab, s, b = jobs[job]
+                batch, s, panel = jobs[job]
                 if j == 0:
-                    hop2_staged[job] = store_pool.tile([P, ROWS, NODES], F32, name="staged")
+                    staging[2, job] = store_pool.tile([P, ROWS, NODES], F32, name="staged")
                 product_to_hbm(
                     hop1_codes[job][:],
                     hop1_scales[job][:],
                     s,
                     j,
-                    hop2_staged[job],
-                    panel_in_hbm(hop2_outs[s], slab, b),
+                    staging[2, job],
+                    hop2_outs[s],
+                    batch,
+                    panel,
                 )
             if n < quarters:
                 job, j = divmod(n, ROWS)
-                slab, s, b = jobs[job]
-                i = job % STEP_PAIRS
+                batch, s, panel = jobs[job]
                 if j == 0:
                     hop1_grouped[job] = hop1_pool.tile(
                         [P, PANEL, PACK], BF16, name="hop1_grouped", align_bytes=64
                     )
-                flipped_first_hop(slab, s, b, j, hop1_grouped[job])
+                flipped_first_hop(batch, s, panel, j, hop1_grouped[job])
                 if j == ROWS - 1:
                     hop1_codes[job] = hop1_pool.tile(
                         [P, PANEL], U32, name="hop1_codes", align_bytes=64
@@ -255,5 +253,13 @@ def tile_adaptivegcn_pb_t_kernel(
                         scales=hop1_scales[job][:],
                         in_=hop1_grouped[job][:].rearrange("p r t -> p (r t)"),
                     )
-                if i == STEP_PAIRS - 1 and j in (1, 2) and slab + 1 < SLABS:
-                    quantise_x(slab + 1, j - 1)
+                if batch + 1 < BATCHES:
+                    g = job % X_BANKS
+                    if j == 0:
+                        if g == 0:
+                            new_batch(batch + 1)
+                        sort_x(nc.vector.tensor_copy, batch + 1, g, flip_x(batch + 1, [g])[g])
+                    if g == X_BANKS - 1 and 1 <= j <= PANELS:
+                        quantise_x(batch + 1, j - 1)
+                if n == ROWS - 1:
+                    quantise_support(1, (nc.scalar.copy, nc.scalar.copy))

@@ -21,7 +21,7 @@ PANEL_STEPS = PANEL // CHANNELS
 PANELS = STEPS // PANEL_STEPS
 X_BANKS = 4
 HALF = NODES // 2
-LAG = 6
+LAG = 4
 
 FLOPS = 4 * 2 * BATCHES * STEPS * CHANNELS * NODES * NODES
 
@@ -38,7 +38,7 @@ def tile_adaptivegcn_pb_t_kernel(
         ctx.enter_context(tc.manual_schedule())
         resident = ctx.enter_context(tc.tile_pool(name="resident", bufs=1))
         x_pool = ctx.enter_context(tc.tile_pool(name="x_pool", bufs=2))
-        hop1_pool = ctx.enter_context(tc.tile_pool(name="hop1_pool", bufs=3))
+        hop1_pool = ctx.enter_context(tc.tile_pool(name="hop1_pool", bufs=LAG + 2))
         store_pool = ctx.enter_context(tc.tile_pool(name="store_pool", bufs=6))
         psum_quant = ctx.enter_context(tc.psum_pool(name="psum_quant", bufs=4))
         psum_store = ctx.enter_context(tc.psum_pool(name="psum_store", bufs=4))
@@ -76,7 +76,7 @@ def tile_adaptivegcn_pb_t_kernel(
         support_codes = {}
         support_scales = {}
 
-        def quantise_support(s, copies):
+        def quantise_support(s):
             grouped = resident.tile(
                 [P, NODES, PACK], BF16, name="support_grouped_%d" % s, align_bytes=64
             )
@@ -89,7 +89,8 @@ def tile_adaptivegcn_pb_t_kernel(
                             support_rows[s][:, 2 * half + g, t * P : (t + 1) * P],
                             ident_bf16[:],
                         )
-                copies[half](
+                copy = nc.vector.tensor_copy if half == 0 else nc.scalar.copy
+                copy(
                     out=grouped[:, half * HALF : (half + 1) * HALF, :],
                     in_=flipped[:].rearrange("p t w -> p w t"),
                 )
@@ -144,29 +145,26 @@ def tile_adaptivegcn_pb_t_kernel(
                 in_=x_grouped[batch][:, panel, :],
             )
 
-        def product_to_hbm(codes, scales, s, j, staged, out, batch, panel):
-            cols = slice(j * P, (j + 1) * P)
+        def product_to_hbm(codes, scales, s, j, staged, out, batch, panel, alone):
             bank = psum_store.tile([P, NODES], F32, tag="store_bank")
             nc.tensor.matmul_mx(
                 out=bank[:],
-                lhsT=codes[:, cols].bitcast(FP8X4),
-                lhsT_scale=scales[:, cols],
+                lhsT=codes.bitcast(FP8X4),
+                lhsT_scale=scales,
                 rhs=support_codes[s][:].bitcast(FP8X4),
                 rhs_scale=support_scales[s][:],
                 start=True,
                 stop=True,
             )
             nc.scalar.copy(out=staged[:, j, :], in_=bank[:])
-            if j == ROWS - 1:
-                first = batch * STEPS + panel * PANEL_STEPS
-                nc.sync.dma_start(
-                    out=out[first : first + PANEL_STEPS].rearrange(
-                        "l (c j) w -> (l c) (j w)", j=ROWS
-                    ),
-                    in_=staged[:].rearrange("p j w -> p (j w)"),
-                )
+            first = batch * STEPS + panel * PANEL_STEPS
+            in_hbm = out[first : first + PANEL_STEPS].rearrange("l (c j) w -> (l c) j w", j=ROWS)
+            if alone:
+                nc.sync.dma_start(out=in_hbm[:, j, :], in_=staged[:, j, :])
+            elif j == ROWS - 1:
+                nc.sync.dma_start(out=in_hbm, in_=staged[:])
 
-        def flipped_first_hop(batch, s, panel, j, grouped):
+        def flipped_first_hop(batch, s, panel, j):
             cols = slice(j * P, (j + 1) * P)
             bank = psum_quant.tile([P, PACK, P], F32, name="hop1_flipped", tag="quant_bank")
             for t in range(PACK):
@@ -180,9 +178,21 @@ def tile_adaptivegcn_pb_t_kernel(
                     start=True,
                     stop=True,
                 )
-            nc.vector.tensor_copy(out=grouped[:, cols, :], in_=bank[:].rearrange("p t r -> p r t"))
+            grouped = hop1_pool.tile([P, P, PACK], BF16, name="hop1_grouped", align_bytes=64)
+            nc.vector.tensor_copy(out=grouped[:], in_=bank[:].rearrange("p t r -> p r t"))
+            return grouped
 
-        quantise_support(0, (nc.vector.tensor_copy, nc.scalar.copy))
+        def quantise_hop1(grouped):
+            codes = hop1_pool.tile([P, P], U32, name="hop1_codes", align_bytes=64)
+            scales = hop1_pool.tile([P, P], U8, name="hop1_scales", align_bytes=64)
+            nc.vector.quantize_mx(
+                out=codes[:].bitcast(FP8X4),
+                scales=scales[:],
+                in_=grouped[:].rearrange("p r t -> p (r t)"),
+            )
+            return codes, scales
+
+        quantise_support(0)
         new_batch(0)
         first_banks = flip_x(0, range(X_BANKS))
         for panel in range(PANELS):
@@ -200,66 +210,48 @@ def tile_adaptivegcn_pb_t_kernel(
         quarters = len(jobs) * ROWS
         staging = {}
         hop1_grouped = {}
-        hop1_codes = {}
-        hop1_scales = {}
+        hop1_quantised = {}
         for n in range(quarters + LAG):
+            alone = n >= quarters - ROWS
             if n < quarters:
                 job, j = divmod(n, ROWS)
                 batch, s, panel = jobs[job]
+                cols = slice(j * P, (j + 1) * P)
                 if j == 0:
                     staging[1, job] = store_pool.tile([P, ROWS, NODES], F32, name="staged")
                 product_to_hbm(
-                    x_codes[batch][:, panel, :],
-                    x_scales[batch][:, panel, :],
+                    x_codes[batch][:, panel, cols],
+                    x_scales[batch][:, panel, cols],
                     s,
                     j,
                     staging[1, job],
                     hop1_outs[s],
                     batch,
                     panel,
+                    alone,
                 )
             if n >= LAG:
                 job, j = divmod(n - LAG, ROWS)
                 batch, s, panel = jobs[job]
+                codes, scales = hop1_quantised[n - LAG]
                 if j == 0:
                     staging[2, job] = store_pool.tile([P, ROWS, NODES], F32, name="staged")
                 product_to_hbm(
-                    hop1_codes[job][:],
-                    hop1_scales[job][:],
-                    s,
-                    j,
-                    staging[2, job],
-                    hop2_outs[s],
-                    batch,
-                    panel,
+                    codes[:], scales[:], s, j, staging[2, job], hop2_outs[s], batch, panel, alone
                 )
             if n < quarters:
                 job, j = divmod(n, ROWS)
                 batch, s, panel = jobs[job]
-                if j == 0:
-                    hop1_grouped[job] = hop1_pool.tile(
-                        [P, PANEL, PACK], BF16, name="hop1_grouped", align_bytes=64
-                    )
-                flipped_first_hop(batch, s, panel, j, hop1_grouped[job])
-                if j == ROWS - 1:
-                    hop1_codes[job] = hop1_pool.tile(
-                        [P, PANEL], U32, name="hop1_codes", align_bytes=64
-                    )
-                    hop1_scales[job] = hop1_pool.tile(
-                        [P, PANEL], U8, name="hop1_scales", align_bytes=64
-                    )
-                    nc.vector.quantize_mx(
-                        out=hop1_codes[job][:].bitcast(FP8X4),
-                        scales=hop1_scales[job][:],
-                        in_=hop1_grouped[job][:].rearrange("p r t -> p (r t)"),
-                    )
-                if batch + 1 < BATCHES:
-                    g = job % X_BANKS
-                    if j == 0:
-                        if g == 0:
-                            new_batch(batch + 1)
-                        sort_x(nc.vector.tensor_copy, batch + 1, g, flip_x(batch + 1, [g])[g])
-                    if g == X_BANKS - 1 and 1 <= j <= PANELS:
-                        quantise_x(batch + 1, j - 1)
+                hop1_grouped[n] = flipped_first_hop(batch, s, panel, j)
+            if 1 <= n <= quarters:
+                hop1_quantised[n - 1] = quantise_hop1(hop1_grouped[n - 1])
+            if n < quarters:
+                g = job % X_BANKS
+                if batch + 1 < BATCHES and j == 0:
+                    if g == 0:
+                        new_batch(batch + 1)
+                    sort_x(nc.vector.tensor_copy, batch + 1, g, flip_x(batch + 1, [g])[g])
+                if batch + 1 < BATCHES and j == 1 and g % 2 == 1:
+                    quantise_x(batch + 1, g // 2)
                 if n == ROWS - 1:
-                    quantise_support(1, (nc.scalar.copy, nc.scalar.copy))
+                    quantise_support(1)

from contextlib import ExitStack

import concourse.mybir as mybir
from concourse.masks import make_identity

BF16 = mybir.dt.bfloat16
F32 = mybir.dt.float32
U32 = mybir.dt.uint32
U8 = mybir.dt.uint8
FP8X4 = mybir.dt.float8_e4m3fn_x4

P = 128
PACK = 4
BATCHES, CHANNELS, NODES, STEPS = 4, 64, 512, 16
assert NODES == P * PACK
assert 2 * CHANNELS == P

ROWS = 4
PANEL = P * ROWS
PANEL_STEPS = PANEL // CHANNELS
PANELS = STEPS // PANEL_STEPS
X_BANKS = 4
HALF = NODES // 2
LAG = 4

FLOPS = 4 * 2 * BATCHES * STEPS * CHANNELS * NODES * NODES


def tile_adaptivegcn_pb_t_kernel(
    tc, x, support0, support1, out_0, out_1, out_2, out_3
):
    nc = tc.nc
    supports = (support0, support1)
    hop1_outs = (out_0, out_2)
    hop2_outs = (out_1, out_3)

    with ExitStack() as ctx:
        ctx.enter_context(tc.manual_schedule())
        resident = ctx.enter_context(tc.tile_pool(name="resident", bufs=1))
        x_pool = ctx.enter_context(tc.tile_pool(name="x_pool", bufs=2))
        hop1_pool = ctx.enter_context(tc.tile_pool(name="hop1_pool", bufs=LAG + 2))
        store_pool = ctx.enter_context(tc.tile_pool(name="store_pool", bufs=6))
        psum_quant = ctx.enter_context(tc.psum_pool(name="psum_quant", bufs=4))
        psum_store = ctx.enter_context(tc.psum_pool(name="psum_store", bufs=4))

        def load_support(s):
            rows = resident.tile([P, PACK, NODES], BF16, name="support_rows_%d" % s)
            nc.sync.dma_start(out=rows[:], in_=supports[s].rearrange("(g p) v -> p g v", p=P))
            return rows

        def load_x(batch):
            rows = x[batch].rearrange("c (h f) -> (c h) f", h=2)
            pieces = []
            for u in range(2):
                piece = resident.tile([P, P * STEPS], BF16, name="x_rows_%d_%d" % (batch, u))
                nc.sync.dma_start(out=piece[:], in_=rows[:, u * P * STEPS : (u + 1) * P * STEPS])
                pieces.append(piece)
            return pieces

        support_rows = {0: load_support(0)}
        x_rows = {0: load_x(0)}
        support_rows[1] = load_support(1)
        for batch in range(1, BATCHES):
            x_rows[batch] = load_x(batch)

        ident_bf16 = resident.tile([P, P], BF16)
        make_identity(nc, ident_bf16[:])
        ident_f32 = resident.tile([P, P], F32)
        make_identity(nc, ident_f32[:])
        sort_channels = resident.tile([P, P], F32)
        nc.vector.tensor_copy(
            out=sort_channels[:].rearrange("q (j c h) -> q j c h", j=ROWS, h=2),
            in_=ident_f32[:].rearrange("q (c j h) -> q j c h", j=ROWS, h=2),
        )

        support_codes = {}
        support_scales = {}

        def quantise_support(s):
            grouped = resident.tile(
                [P, NODES, PACK], BF16, name="support_grouped_%d" % s, align_bytes=64
            )
            for half in range(2):
                flipped = psum_store.tile([P, PACK, HALF], BF16, tag="store_bank")
                for t in range(PACK):
                    for g in range(2):
                        nc.tensor.transpose(
                            flipped[:, t, g * P : (g + 1) * P],
                            support_rows[s][:, 2 * half + g, t * P : (t + 1) * P],
                            ident_bf16[:],
                        )
                copy = nc.vector.tensor_copy if half == 0 else nc.scalar.copy
                copy(
                    out=grouped[:, half * HALF : (half + 1) * HALF, :],
                    in_=flipped[:].rearrange("p t w -> p w t"),
                )
            support_codes[s] = resident.tile(
                [P, NODES], U32, name="support_codes_%d" % s, align_bytes=64
            )
            support_scales[s] = resident.tile(
                [P, NODES], U8, name="support_scales_%d" % s, align_bytes=64
            )
            nc.vector.quantize_mx(
                out=support_codes[s][:].bitcast(FP8X4),
                scales=support_scales[s][:],
                in_=grouped[:].rearrange("p w t -> p (w t)"),
            )

        x_grouped = {}
        x_codes = {}
        x_scales = {}

        def new_batch(batch):
            x_grouped[batch] = x_pool.tile(
                [P, PANELS, PANEL * PACK], BF16, name="x_grouped", align_bytes=64
            )
            x_codes[batch] = x_pool.tile([P, PANELS, PANEL], U32, name="x_codes", align_bytes=64)
            x_scales[batch] = x_pool.tile([P, PANELS, PANEL], U8, name="x_scales", align_bytes=64)

        def flip_x(batch, which_banks):
            banks = {}
            for g in which_banks:
                banks[g] = psum_quant.tile([P, 2, 2, P], F32, name="x_flipped", tag="quant_bank")
            for u in range(2):
                words = x_rows[batch][u][:].bitcast(F32).rearrange("q (k w) -> q k w", w=STEPS // 2)
                for g in which_banks:
                    for i in range(2):
                        nc.tensor.transpose(
                            banks[g][:, i, u, :], words[:, :, 2 * g + i], sort_channels[:]
                        )
            return banks

        def sort_x(copy, batch, g, bank):
            halves = bank[:].bitcast(BF16).rearrange("p i u (j m e) -> p e i j m u", j=ROWS, e=2)
            sorted_steps = x_grouped[batch][:, g // 2, :].rearrange(
                "p (j a i e m u) -> p a e i j m u", j=ROWS, a=2, i=2, e=2, u=2
            )
            for e in range(2):
                copy(out=sorted_steps[:, g % 2, e], in_=halves[:, e])

        def quantise_x(batch, panel):
            nc.vector.quantize_mx(
                out=x_codes[batch][:, panel, :].bitcast(FP8X4),
                scales=x_scales[batch][:, panel, :],
                in_=x_grouped[batch][:, panel, :],
            )

        def product_to_hbm(codes, scales, s, j, staged, out, batch, panel, alone):
            bank = psum_store.tile([P, NODES], F32, tag="store_bank")
            nc.tensor.matmul_mx(
                out=bank[:],
                lhsT=codes.bitcast(FP8X4),
                lhsT_scale=scales,
                rhs=support_codes[s][:].bitcast(FP8X4),
                rhs_scale=support_scales[s][:],
                start=True,
                stop=True,
            )
            nc.scalar.copy(out=staged[:, j, :], in_=bank[:])
            first = batch * STEPS + panel * PANEL_STEPS
            in_hbm = out[first : first + PANEL_STEPS].rearrange("l (c j) w -> (l c) j w", j=ROWS)
            if alone:
                nc.sync.dma_start(out=in_hbm[:, j, :], in_=staged[:, j, :])
            elif j == ROWS - 1:
                nc.sync.dma_start(out=in_hbm, in_=staged[:])

        def flipped_first_hop(batch, s, panel, j):
            cols = slice(j * P, (j + 1) * P)
            bank = psum_quant.tile([P, PACK, P], F32, name="hop1_flipped", tag="quant_bank")
            for t in range(PACK):
                nodes = slice(t * P, (t + 1) * P)
                nc.tensor.matmul_mx(
                    out=bank[:, t, :],
                    lhsT=support_codes[s][:, nodes].bitcast(FP8X4),
                    lhsT_scale=support_scales[s][:, nodes],
                    rhs=x_codes[batch][:, panel, cols].bitcast(FP8X4),
                    rhs_scale=x_scales[batch][:, panel, cols],
                    start=True,
                    stop=True,
                )
            grouped = hop1_pool.tile([P, P, PACK], BF16, name="hop1_grouped", align_bytes=64)
            nc.vector.tensor_copy(out=grouped[:], in_=bank[:].rearrange("p t r -> p r t"))
            return grouped

        def quantise_hop1(grouped):
            codes = hop1_pool.tile([P, P], U32, name="hop1_codes", align_bytes=64)
            scales = hop1_pool.tile([P, P], U8, name="hop1_scales", align_bytes=64)
            nc.vector.quantize_mx(
                out=codes[:].bitcast(FP8X4),
                scales=scales[:],
                in_=grouped[:].rearrange("p r t -> p (r t)"),
            )
            return codes, scales

        quantise_support(0)
        new_batch(0)
        first_banks = flip_x(0, range(X_BANKS))
        for panel in range(PANELS):
            sort_x(nc.vector.tensor_copy, 0, 2 * panel, first_banks[2 * panel])
            sort_x(nc.scalar.copy, 0, 2 * panel + 1, first_banks[2 * panel + 1])
            quantise_x(0, panel)

        jobs = [
            (batch, s, panel)
            for batch in range(BATCHES)
            for s in range(2)
            for panel in range(PANELS)
        ]
        assert len(jobs) == BATCHES * X_BANKS
        quarters = len(jobs) * ROWS
        staging = {}
        hop1_grouped = {}
        hop1_quantised = {}
        for n in range(quarters + LAG):
            alone = n >= quarters - ROWS
            if n < quarters:
                job, j = divmod(n, ROWS)
                batch, s, panel = jobs[job]
                cols = slice(j * P, (j + 1) * P)
                if j == 0:
                    staging[1, job] = store_pool.tile([P, ROWS, NODES], F32, name="staged")
                product_to_hbm(
                    x_codes[batch][:, panel, cols],
                    x_scales[batch][:, panel, cols],
                    s,
                    j,
                    staging[1, job],
                    hop1_outs[s],
                    batch,
                    panel,
                    alone,
                )
            if n >= LAG:
                job, j = divmod(n - LAG, ROWS)
                batch, s, panel = jobs[job]
                codes, scales = hop1_quantised[n - LAG]
                if j == 0:
                    staging[2, job] = store_pool.tile([P, ROWS, NODES], F32, name="staged")
                product_to_hbm(
                    codes[:], scales[:], s, j, staging[2, job], hop2_outs[s], batch, panel, alone
                )
            if n < quarters:
                job, j = divmod(n, ROWS)
                batch, s, panel = jobs[job]
                hop1_grouped[n] = flipped_first_hop(batch, s, panel, j)
            if 1 <= n <= quarters:
                hop1_quantised[n - 1] = quantise_hop1(hop1_grouped[n - 1])
            if n < quarters:
                g = job % X_BANKS
                if batch + 1 < BATCHES and j == 0:
                    if g == 0:
                        new_batch(batch + 1)
                    sort_x(nc.vector.tensor_copy, batch + 1, g, flip_x(batch + 1, [g])[g])
                if batch + 1 < BATCHES and j == 1 and g % 2 == 1:
                    quantise_x(batch + 1, g // 2)
                if n == ROWS - 1:
                    quantise_support(1)
